import numpy as np
import ml_dtypes


def mxq(x, axis, fmt="e4m3"):
    dtype, down = {"e4m3": (ml_dtypes.float8_e4m3fn, 7), "e5m2": (ml_dtypes.float8_e5m2, 14)}[fmt]
    v = np.moveaxis(np.asarray(x, np.float32).astype(ml_dtypes.bfloat16).astype(np.float64), axis, -1)
    blocks = v.reshape(v.shape[:-1] + (-1, 32))
    amax = np.abs(blocks).max(-1, keepdims=True)
    byte = np.maximum(np.where(amax > 0, np.frexp(amax)[1] - 1 + 127, 0) - down, 1)
    scale = np.exp2(byte - 127.0)
    codes = (blocks / scale).astype(np.float32).astype(dtype).astype(np.float64)
    return np.moveaxis((codes * scale).reshape(v.shape), -1, axis)


WIDE = False


def mx_kscale(k):
    if not WIDE:
        return np.ones(k)
    levels = np.array([10, -10, 5, -5, 0])
    if k % 512:
        return np.exp2(np.random.permutation(np.resize(levels, k // 32))).repeat(32)
    a = np.empty((k // 512, 16))
    for p in range(k // 512):
        a[p, :8] = np.random.permutation(np.resize(levels, 8))
        for g in range(8):
            far = levels[np.abs(levels - a[p, g]) >= 10]
            a[p, g + 8] = far[np.random.randint(len(far))]
    return np.exp2(a.ravel()).repeat(32)


BF16 = ml_dtypes.bfloat16


def bf(x):
    return np.asarray(x, np.float32).astype(BF16)


def f64(x):
    return np.asarray(x).astype(np.float64)


E2M1 = np.array([0.0, 0.5, 1.0, 1.5, 2.0, 3.0, 4.0, 6.0, -0.0, -0.5, -1.0, -1.5, -2.0, -3.0, -4.0, -6.0])


def pack_weight(w, fmt):
    k, n = w.shape
    w = f64(bf(w)).reshape(k // 32, 32, n)
    amax = np.abs(w).max(1)
    if fmt == "e4m3":
        byte = np.frexp(amax)[1] - 1 + 127 - 7
    else:
        mant, ex = np.frexp(amax / 6.0)
        byte = np.where(mant > 0.5, ex, ex - 1) + 127
    byte = np.clip(np.where(amax > 0, byte, 1), 1, 254)
    scaled = (w * np.exp2(127.0 - byte)[:, None, :]).reshape(k, n).astype(np.float32)
    by_word = np.ascontiguousarray(scaled.reshape(k // 512, 128, 4, n).transpose(0, 1, 3, 2))
    if fmt == "e4m3":
        words = by_word.astype(ml_dtypes.float8_e4m3fn).view(np.uint8)
    else:
        c = by_word.astype(ml_dtypes.float4_e2m1fn).view(np.uint8) & 0xF
        words = c[..., 0::2] | (c[..., 1::2] << 4)
    return np.ascontiguousarray(words), np.ascontiguousarray(byte.astype(np.uint8).reshape(k // 512, 16, n))


def unpack_weight(words, scales, fmt):
    g, p, n, _ = words.shape
    if fmt == "e4m3":
        vals = np.ascontiguousarray(words).view(ml_dtypes.float8_e4m3fn).astype(np.float64)
    else:
        nib = np.empty((g, p, n, 4), np.uint8)
        nib[..., 0::2] = words & 0xF
        nib[..., 1::2] = words >> 4
        vals = E2M1[nib]
    vals = vals * np.repeat(np.exp2(scales.astype(np.float64) - 127.0), 8, axis=1)[..., None]
    return vals.transpose(0, 1, 3, 2).reshape(g * 512, n)


B, S, HID, H, R, VR, KVR, QLR, HD = 1, 512, 2048, 4, 128, 128, 512, 1536, 128
ROPE_BASE = 10000.0


def rotate_half(x):
    half = x.shape[-1] // 2
    return np.concatenate([-x[..., half:], x[..., :half]], axis=-1)


def rope_tables():
    inv_freq = 1.0 / ROPE_BASE ** (np.arange(0, R, 2) / R)
    freqs = np.outer(np.arange(S), inv_freq)
    emb = np.concatenate([freqs, freqs], axis=-1)
    return np.broadcast_to(np.cos(emb), (B, S, R)), np.broadcast_to(np.sin(emb), (B, S, R))


def draw0():
    s, t = mx_kscale(HID), mx_kscale(QLR)
    cos, sin = rope_tables()
    hidden_states = bf(np.random.standard_normal((B, S, HID)) * s)
    w_qa_words, w_qa_scales = pack_weight((np.random.standard_normal((QLR, HID)) / np.sqrt(HID) * t[:, None] / s[None, :]).T, "e4m3")
    w_qb_words, w_qb_scales = pack_weight((np.random.standard_normal((H * (R + KVR), QLR)) / np.sqrt(QLR) / t[None, :]).T, "e4m3")
    w_kv_words, w_kv_scales = pack_weight((np.random.standard_normal((R + VR + KVR, HID)) / np.sqrt(HID) / s[None, :]).T, "e4m3")
    return {"hidden_states": hidden_states,
            "cos": bf(cos), "sin": bf(sin),
            "w_qa_words": w_qa_words, "w_qa_scales": w_qa_scales,
            "w_qb_words": w_qb_words, "w_qb_scales": w_qb_scales,
            "w_kv_words": w_kv_words, "w_kv_scales": w_kv_scales}


def core(hidden_states, cos, sin, w_qa_words, w_qa_scales, w_qb_words, w_qb_scales, w_kv_words, w_kv_scales):
    c, sn = f64(cos), f64(sin)
    hq = mxq(f64(hidden_states), 2, "e4m3")
    q_lora = hq @ unpack_weight(w_qa_words, w_qa_scales, "e4m3")
    q = (mxq(q_lora, 2, "e4m3") @ unpack_weight(w_qb_words, w_qb_scales, "e4m3")).reshape(B, S, H, R + KVR)
    kv = hq @ unpack_weight(w_kv_words, w_kv_scales, "e4m3")
    q_rope = q[..., :R].transpose(0, 2, 1, 3)
    q_rope = q_rope * c[:, None] + rotate_half(q_rope) * sn[:, None]
    q_nope = q[..., R:].transpose(0, 2, 1, 3)
    k_rope = kv[..., :R]
    k_rope = k_rope * c + rotate_half(k_rope) * sn
    v_rope = kv[..., R:R + VR]
    kv_nope = kv[..., R + VR:]
    return q_rope, q_nope, k_rope, v_rope, kv_nope


def e4m3fn_bytes(y):
    return np.clip(np.asarray(y, np.float64), -448.0, 448.0).astype(np.float32).astype(ml_dtypes.float8_e4m3fn).view(np.uint8)


def e4m3fn_values(b):
    return np.asarray(b, np.uint8).view(ml_dtypes.float8_e4m3fn).astype(np.float64)


def setup_inputs():
    d = draw0()
    x0 = np.asarray(d['hidden_states']).astype(np.float64)
    s = (np.max(np.abs(x0), axis=(0, 1), keepdims=True) / 448.0).astype(np.float32)
    out = {}
    for k, v in d.items():
        if k == 'hidden_states':
            out['hidden_states_bytes'] = e4m3fn_bytes(x0 / s.astype(np.float64))
            out['hidden_states_scale'] = s
        else:
            out[k] = v
    return out


def reference(hidden_states_bytes, hidden_states_scale, cos, sin, w_qa_words, w_qa_scales, w_qb_words, w_qb_scales, w_kv_words, w_kv_scales):
    return core(e4m3fn_values(hidden_states_bytes) * hidden_states_scale.astype(np.float64), cos, sin, w_qa_words, w_qa_scales, w_qb_words, w_qb_scales, w_kv_words, w_kv_scales)

@@ -1,0 +1,365 @@
+from contextlib import ExitStack
+
+import concourse.mybir as mybir
+from concourse.masks import make_identity
+
+F32 = mybir.dt.float32
+BF16 = mybir.dt.bfloat16
+U32 = mybir.dt.uint32
+I32 = mybir.dt.int32
+U8 = mybir.dt.uint8
+FP8 = mybir.dt.float8_e4m3fn
+FP8X4 = mybir.dt.float8_e4m3fn_x4
+MULT = mybir.AluOpType.mult
+ADD = mybir.AluOpType.add
+
+P = 128
+TOK = 512
+HID = 2048
+QLR = 1536
+HEADS = 4
+KV = 768
+FLOPS = 2 * TOK * (HID * QLR + QLR * HEADS * 640 + HID * KV)
+
+
+def tile_absorbqkvo_pa_w8_kernel(
+    tc, x_bytes, x_scale, cos, sin, qa_words, qa_scales, qb_words, qb_scales, kv_words, kv_scales,
+    q_rope, q_nope, k_rope, v_rope, kv_nope,
+):
+    nc = tc.nc
+    with ExitStack() as ctx:
+        keep = ctx.enter_context(tc.tile_pool(name="keep", bufs=1))
+        tmp = ctx.enter_context(tc.tile_pool(name="tmp", bufs=2))
+        psum = ctx.enter_context(tc.psum_pool(name="psum", bufs=8))
+        ctx.enter_context(tc.manual_schedule())
+
+        ident = keep.tile([P, P], F32, name="ident")
+        warm = keep.tile([P, 1], F32, name="warm")
+        xin = keep.tile([P, 4, HID], U8, name="xin", align_bytes=64)
+        xsc = keep.tile([P, 16], F32, name="xsc")
+        cs = keep.tile([P, 4, 128], BF16, name="cs", align_bytes=64)
+        sn = keep.tile([P, 4, 128], BF16, name="sn", align_bytes=64)
+        kvw = keep.tile([P, 4, KV], U32, name="kvw", align_bytes=64)
+        kvs = keep.tile([P, KV], U8, name="kvs", align_bytes=64)
+        qaw = keep.tile([P, 3, 4, 512], U32, name="qaw", align_bytes=64)
+        qas = keep.tile([P, QLR], U8, name="qas", align_bytes=64)
+        qbr = keep.tile([P, 3, 512], U32, name="qbr", align_bytes=64)
+        qbrs = keep.tile([P, 512], U8, name="qbrs", align_bytes=64)
+        qbn = keep.tile([P, 3, 4, 512], U32, name="qbn", align_bytes=64)
+        qbs = keep.tile([P, HEADS * 640], U8, name="qbs", align_bytes=64)
+        xb = keep.tile([P, 4, HID], BF16, name="xb", align_bytes=64)
+        xg = keep.tile([P, 4, HID], BF16, name="xg", align_bytes=64)
+        xc = keep.tile([P, 4 * 512], U32, name="xc", align_bytes=64)
+        xs = keep.tile([P, 4 * 512], U8, name="xs", align_bytes=64)
+        ql = keep.tile([P, 4, 512], BF16, name="ql", align_bytes=64)
+        qp = keep.tile([P, 2, 4, TOK], BF16, name="qp", align_bytes=64)
+        qg = keep.tile([P, 3, TOK * 4], BF16, name="qg", align_bytes=64)
+        qc = keep.tile([P, 3 * TOK], U32, name="qc", align_bytes=64)
+        qs = keep.tile([P, 3 * TOK], U8, name="qs", align_bytes=64)
+        qap = keep.tile([P, 2, 4, 512], U32, name="qap", align_bytes=64)
+        qaps = keep.tile([P, 2, 512], U8, name="qaps", align_bytes=64)
+        zero = keep.tile([P, 512], BF16, name="zero")
+        kvn_o = keep.tile([P, 4, 512], F32, name="kvn_o")
+        kvr_o = keep.tile([P, 4, 256], F32, name="kvr_o")
+        kr_o = keep.tile([P, 4, 128], F32, name="kr_o")
+        qr_o = keep.tile([P, 4, 512], F32, name="qr_o")
+        qn_o = keep.tile([P, 4, 4, 512], F32, name="qn_o")
+
+        nc.vector.memset(zero[:], 0.0)
+        nc.vector.memset(warm[:], 0.0)
+        nc.vector.memset(kvs[:].bitcast(I32), 0)
+        nc.vector.memset(qas[:].bitcast(I32), 0)
+        nc.vector.memset(qbs[:].bitcast(I32), 0)
+        make_identity(nc, ident[:])
+        nc.scalar.dma_start(out=xsc[:].rearrange("p (g t) -> p g t", t=4), in_=x_scale[0, 0, :].rearrange("(g p t) -> p g t", p=P, t=4))
+        nc.scalar.copy(out=warm[:], in_=warm[:])
+
+        def load_x(j):
+            nc.sync.dma_start(out=xin[:, j, :], in_=x_bytes[0, P * j : P * (j + 1), :])
+
+        def load_scales(tile, src, groups):
+            for q in range(4):
+                nc.sync.dma_start(out=tile[32 * q : 32 * q + 4 * groups, :].bitcast(I32), in_=src[:, 4 * q : 4 * q + 4, :].bitcast(I32))
+
+        def load_qa(c):
+            nc.sync.dma_start(out=qaw[:, c, :, :].bitcast(I32), in_=qa_words[:, :, 512 * c : 512 * (c + 1), :].rearrange("g p n t -> p g (n t)").bitcast(I32))
+
+        load_x(0)
+        load_scales(kvs, kv_scales, 4)
+        load_scales(qas, qa_scales, 4)
+        load_x(1)
+        for g in range(0, 4, 2):
+            nc.sync.dma_start(out=kvw[:, g : g + 2, :].bitcast(I32), in_=kv_words[g : g + 2].rearrange("g p n t -> p g (n t)").bitcast(I32))
+        load_x(2)
+        load_qa(0)
+        load_x(3)
+        load_qa(1)
+        load_qa(2)
+        nc.sync.dma_start(out=cs[:], in_=cos[0].rearrange("(j p) d -> p j d", p=P))
+        nc.sync.dma_start(out=sn[:], in_=sin[0].rearrange("(j p) d -> p j d", p=P))
+        load_scales(qbs, qb_scales, 3)
+        for g in range(3):
+            wg = qb_words[g].rearrange("p (h n) t -> p h n t", h=HEADS)
+            nc.sync.dma_start(out=qbr[:, g, :].rearrange("p (h n) -> p h n", h=HEADS).bitcast(I32), in_=wg[:, :, 0:128, :].rearrange("p h n t -> p h (n t)").bitcast(I32))
+        for g in range(3):
+            wg = qb_words[g].rearrange("p (h n) t -> p h n t", h=HEADS)
+            nc.sync.dma_start(out=qbn[:, g, :, :].bitcast(I32), in_=wg[:, :, 128:640, :].rearrange("p h n t -> p h (n t)").bitcast(I32))
+        nc.gpsimd.tensor_scalar(out=sn[:, :, 0:64], in0=sn[:, :, 0:64], scalar1=-1.0, scalar2=0.0, op0=MULT, op1=ADD)
+
+        def bank():
+            return psum.tile([P, 512], F32, name="bank", tag="bank")
+
+        dummy = bank()
+
+        def warm_up(n):
+            for i in range(n):
+                nc.tensor.matmul(dummy[:], lhsT=zero[:, 0:128], rhs=zero[:], start=True, stop=True)
+
+        def cast_x(eng, j, a, b):
+            dst, src = xb[:, j, a:b], xin[:, j, a:b].bitcast(FP8)
+            if eng == "v":
+                nc.vector.tensor_copy(out=dst, in_=src)
+            else:
+                nc.scalar.copy(out=dst, in_=src)
+
+        xt = {}
+
+        def transpose_x(j, halves=(0, 1)):
+            words = xb[:, j, :].bitcast(F32)
+            for half in halves:
+                t = bank()
+                for gg in range(2):
+                    g = 2 * half + gg
+                    for u in range(2):
+                        o = 256 * gg + 128 * u
+                        nc.tensor.transpose(t[:, o : o + 128], words[:, 256 * g + u : 256 * (g + 1) : 2], ident[:])
+                    xt[j, g] = t[:, 256 * gg : 256 * (gg + 1)]
+
+        def scale_x(j, g):
+            nc.vector.tensor_tensor(
+                out=xg[:, j, 512 * g : 512 * (g + 1)].rearrange("p (r u e) -> p r u e", u=2, e=2),
+                in0=xt[j, g].bitcast(BF16).rearrange("p (u r e) -> p r u e", u=2, e=2),
+                in1=xsc[:, 4 * g : 4 * g + 4].rearrange("p (o u e) -> p o u e", o=1, u=2).to_broadcast([P, P, 2, 2]),
+                op=MULT,
+            )
+
+        def quant_x(j, g):
+            a = 512 * g + 128 * j
+            nc.vector.quantize_mx(out=xc[:, a : a + 128].bitcast(FP8X4), scales=xs[:, a : a + 128], in_=xg[:, j, 512 * g : 512 * (g + 1)])
+
+        def mm(out, codes, scales, a, w, wsc, g, start, stop):
+            nc.tensor.matmul_mx(
+                out=out, lhsT=codes[:, a : a + 128].bitcast(FP8X4), lhsT_scale=scales[:, a : a + 128],
+                rhs=w.bitcast(FP8X4), rhs_scale=wsc, start=start, stop=stop,
+            )
+
+        def kv_block(j):
+            n, r = bank(), bank()
+            for g in range(4):
+                a = 512 * g + 128 * j
+                mm(n[:], xc, xs, a, kvw[:, g, 256:768], kvs[4 * g : P, 256:768], g, g == 0, g == 3)
+                mm(r[:, 0:256], xc, xs, a, kvw[:, g, 0:256], kvs[4 * g : P, 0:256], g, g == 0, g == 3)
+            nc.scalar.copy(out=kvn_o[:, j, :], in_=n[:])
+            nc.scalar.copy(out=kvr_o[:, j, :], in_=r[:, 0:256])
+
+        def qa_tokens(j):
+            t = bank()
+            for g in range(4):
+                mm(t[:], xc, xs, 512 * g + 128 * j, qaw[:, 0, g, :], qas[4 * g : P, 0:512], g, g == 0, g == 3)
+            nc.scalar.copy(
+                out=ql[:, j, :].rearrange("p (u w e) -> p u w e", u=2, e=2),
+                in_=t[:].rearrange("p (w u e) -> p u w e", u=2, e=2),
+            )
+
+        def permute_qa(c, ts):
+            for t in ts:
+                nc.vector.tensor_copy(
+                    out=qap[:, c - 1, :, 128 * t : 128 * (t + 1)].bitcast(I32),
+                    in_=qaw[:, c, :, t:512:4].bitcast(I32),
+                )
+                if t == 0:
+                    nc.vector.tensor_copy(
+                        out=qaps[:, c - 1, :].rearrange("p (t m) -> p m t", t=4),
+                        in_=qas[:, 512 * c : 512 * (c + 1)].rearrange("p (m t) -> p m t", t=4),
+                    )
+
+        def qa_channels(c, t):
+            b = bank()
+            for g in range(4):
+                nc.tensor.matmul_mx(
+                    out=b[:], lhsT=qap[:, c - 1, g, 128 * t : 128 * (t + 1)].bitcast(FP8X4),
+                    lhsT_scale=qaps[4 * g : P, c - 1, 128 * t : 128 * (t + 1)],
+                    rhs=xc[:, 512 * g : 512 * (g + 1)].bitcast(FP8X4), rhs_scale=xs[:, 512 * g : 512 * (g + 1)],
+                    start=g == 0, stop=g == 3,
+                )
+            nc.scalar.copy(out=qp[:, c - 1, t, :], in_=b[:])
+
+        def interleave_q(c, a, n):
+            nc.vector.tensor_copy(
+                out=qg[:, c, 4 * a : 4 * (a + n)].rearrange("p (r i t) -> p r t i", i=4, t=4),
+                in_=qp[:, c - 1, :, a : a + n].rearrange("p t (r i) -> p r t i", i=4),
+            )
+
+        def quant_q(c, a, n):
+            o = TOK * c + a
+            nc.vector.quantize_mx(out=qc[:, o : o + n].bitcast(FP8X4), scales=qs[:, o : o + n], in_=qg[:, c, 4 * a : 4 * (a + n)])
+
+        def transpose_q(pr):
+            t = bank()
+            for jj in range(2):
+                words = ql[:, 2 * pr + jj, :].bitcast(F32)
+                for u in range(2):
+                    o = 256 * jj + 128 * u
+                    nc.tensor.transpose(t[:, o : o + 128], words[:, 128 * u : 128 * (u + 1)], ident[:])
+            return t
+
+        def copy_q(pr, t):
+            nc.vector.tensor_copy(
+                out=qg[:, 0, 1024 * pr : 1024 * (pr + 1)].bitcast(F32).rearrange("p (j r u) -> p j r u", j=2, u=2),
+                in_=t[:].rearrange("p (j u r) -> p j r u", j=2, u=2),
+            )
+
+        def qb_pass(t, j, w, sc, c):
+            mm(t[:], qc, qs, TOK * c + 128 * j, w[:, c], sc[4 * c : P, :], c, c == 0, c == 2)
+
+        def qb_block(j, split):
+            ws = [(qbr, qbrs[:])] + [(qbn[:, :, h, :], qbs[:, 640 * h + 128 : 640 * (h + 1)]) for h in range(HEADS)]
+            tiles = [bank() for w in ws] if split else []
+            if split:
+                for c in range(2):
+                    for t, (w, sc) in zip(tiles, ws):
+                        qb_pass(t, j, w, sc, c)
+
+            def group(i):
+                t = tiles[i] if split else bank()
+                for c in range(2 if split else 0, 3):
+                    qb_pass(t, j, ws[i][0], ws[i][1], c)
+                return t
+
+            t = group(0)
+            r3 = t[:].rearrange("p (h d) -> p h d", h=HEADS)
+            ta = tmp.tile([P, HEADS, 128], F32, name="ta", tag="ta")
+            tb = tmp.tile([P, HEADS, 128], F32, name="tb", tag="tb")
+            nc.vector.tensor_tensor(out=ta[:], in0=r3, in1=cs[:, j : j + 1, :].to_broadcast([P, HEADS, 128]), op=MULT)
+            nc.vector.tensor_tensor(out=tb[:, :, 0:64], in0=r3[:, :, 64:128], in1=sn[:, j : j + 1, 0:64].to_broadcast([P, HEADS, 64]), op=MULT)
+            nc.vector.tensor_tensor(out=tb[:, :, 64:128], in0=r3[:, :, 0:64], in1=sn[:, j : j + 1, 64:128].to_broadcast([P, HEADS, 64]), op=MULT)
+            nc.vector.tensor_tensor(out=qr_o[:, j, :].rearrange("p (h d) -> p h d", h=HEADS), in0=ta[:], in1=tb[:], op=ADD)
+            nc.sync.dma_start(out=q_rope[0, :, P * j : P * (j + 1), :].rearrange("h p d -> p h d"), in_=qr_o[:, j, :].rearrange("p (h d) -> p h d", h=HEADS))
+            for h in range(HEADS):
+                if j == 3 and h == 3:
+                    halves = [bank(), bank()]
+                    for i, t in enumerate(halves):
+                        for c in range(3):
+                            mm(t[:, 0:256], qc, qs, TOK * c + 128 * j, qbn[:, c, h, 256 * i : 256 * (i + 1)],
+                               qbs[4 * c : P, 640 * h + 128 + 256 * i : 640 * h + 384 + 256 * i], c, c == 0, c == 2)
+                    for i, t in enumerate(halves):
+                        o = qn_o[:, j, h, 256 * i : 256 * (i + 1)]
+                        if i == 0:
+                            nc.vector.tensor_copy(out=o, in_=t[:, 0:256])
+                        else:
+                            nc.scalar.copy(out=o, in_=t[:, 0:256])
+                        nc.sync.dma_start(out=q_nope[0, h, P * j : P * (j + 1), 256 * i : 256 * (i + 1)], in_=o)
+                    continue
+                t = group(1 + h)
+                if h == 3:
+                    nc.vector.tensor_copy(out=qn_o[:, j, h, :], in_=t[:])
+                else:
+                    nc.scalar.copy(out=qn_o[:, j, h, :], in_=t[:])
+                nc.sync.dma_start(out=q_nope[0, h, P * j : P * (j + 1), :], in_=qn_o[:, j, h, :])
+
+        def rope_k():
+            ra = tmp.tile([P, 4, 128], F32, name="ra", tag="ta")
+            rb = tmp.tile([P, 4, 128], F32, name="rb", tag="tb")
+            nc.vector.tensor_tensor(out=ra[:], in0=kvr_o[:, :, 0:128], in1=cs[:], op=MULT)
+            nc.vector.tensor_tensor(out=rb[:, :, 0:64], in0=kvr_o[:, :, 64:128], in1=sn[:, :, 0:64], op=MULT)
+            nc.vector.tensor_tensor(out=rb[:, :, 64:128], in0=kvr_o[:, :, 0:64], in1=sn[:, :, 64:128], op=MULT)
+            nc.vector.tensor_tensor(out=kr_o[:], in0=ra[:], in1=rb[:], op=ADD)
+            nc.sync.dma_start(out=k_rope[0].rearrange("(j p) d -> p j d", p=P), in_=kr_o[:])
+
+        warm_up(6)
+        for g in range(4):
+            cast_x("v" if g % 2 == 0 else "s", 0, 512 * g, 512 * (g + 1))
+        transpose_x(0)
+        warm_up(2)
+        scale_x(0, 0)
+        scale_x(0, 1)
+        quant_x(0, 0)
+        scale_x(0, 2)
+        quant_x(0, 1)
+        scale_x(0, 3)
+        quant_x(0, 2)
+        cast_x("s", 1, 0, 1024)
+        cast_x("s", 1, 1024, 2048)
+        transpose_x(1, (0,))
+        warm_up(2)
+        transpose_x(1, (1,))
+        scale_x(1, 0)
+        quant_x(0, 3)
+        cast_x("s", 2, 0, 1024)
+        cast_x("s", 2, 1024, 2048)
+        kv_block(0)
+        scale_x(1, 1)
+        quant_x(1, 0)
+        scale_x(1, 2)
+        quant_x(1, 1)
+        scale_x(1, 3)
+        quant_x(1, 2)
+        transpose_x(2)
+        scale_x(2, 0)
+        quant_x(1, 3)
+        cast_x("s", 3, 0, 1024)
+        cast_x("s", 3, 1024, 2048)
+        qa_tokens(0)
+        kv_block(1)
+        scale_x(2, 1)
+        quant_x(2, 0)
+        scale_x(2, 2)
+        quant_x(2, 1)
+        scale_x(2, 3)
+        quant_x(2, 2)
+        qa_tokens(1)
+        transpose_x(3)
+        scale_x(3, 0)
+        quant_x(2, 3)
+        scale_x(3, 1)
+        quant_x(3, 0)
+        scale_x(3, 2)
+        quant_x(3, 1)
+        scale_x(3, 3)
+        quant_x(3, 2)
+        permute_qa(1, (0,))
+        quant_x(3, 3)
+        permute_qa(1, (1, 2, 3))
+        kv_block(2)
+        qa_tokens(2)
+        permute_qa(2, (0, 1, 2, 3))
+        kv_block(3)
+        qa_tokens(3)
+        nc.vector.tensor_copy(out=qbrs[:].rearrange("p (h n) -> p h n", h=HEADS).bitcast(I32), in_=qbs[:].rearrange("p (h n) -> p h n", h=HEADS)[:, :, 0:128].bitcast(I32))
+        nc.sync.dma_start(out=kv_nope[0].rearrange("(j p) d -> p j d", p=P), in_=kvn_o[:])
+        nc.sync.dma_start(out=v_rope[0].rearrange("(j p) d -> p j d", p=P), in_=kvr_o[:, :, 128:256])
+        for t in range(4):
+            qa_channels(1, t)
+        ta0 = transpose_q(0)
+        ta1 = transpose_q(1)
+        for t in range(4):
+            qa_channels(2, t)
+        copy_q(0, ta0)
+        copy_q(1, ta1)
+        quant_q(0, 0, 256)
+        interleave_q(1, 0, 256)
+        quant_q(0, 256, 256)
+        interleave_q(1, 256, 256)
+        quant_q(1, 0, 256)
+        quant_q(1, 256, 256)
+        interleave_q(2, 0, 128)
+        interleave_q(2, 128, 128)
+        quant_q(2, 0, 128)
+        interleave_q(2, 256, 256)
+        quant_q(2, 128, 128)
+        quant_q(2, 256, 256)
+        qb_block(0, True)
+        rope_k()
+        qb_block(1, False)
+        qb_block(2, False)
+        qb_block(3, False)

@@ -84,15 +84,21 @@ def tile_absorbqkvo_pa_w8_kernel(
         def load_qa(c):
             nc.sync.dma_start(out=qaw[:, c, :, :].bitcast(I32), in_=qa_words[:, :, 512 * c : 512 * (c + 1), :].rearrange("g p n t -> p g (n t)").bitcast(I32))
 
-        load_x(0)
-        load_scales(kvs, kv_scales, 4)
-        load_scales(qas, qa_scales, 4)
+        def load_kv(g):
+            nc.sync.dma_start(out=kvw[:, g, :].bitcast(I32), in_=kv_words[g].rearrange("p n t -> p (n t)").bitcast(I32))
+
+        for a in range(0, HID, HID // 2):
+            nc.sync.dma_start(out=xin[:, 0, a : a + HID // 2], in_=x_bytes[0, 0:P, a : a + HID // 2])
         load_x(1)
-        for g in range(0, 4, 2):
-            nc.sync.dma_start(out=kvw[:, g : g + 2, :].bitcast(I32), in_=kv_words[g : g + 2].rearrange("g p n t -> p g (n t)").bitcast(I32))
+        load_scales(kvs, kv_scales, 4)
+        load_kv(0)
+        load_kv(1)
         load_x(2)
-        load_qa(0)
+        load_kv(2)
+        load_kv(3)
+        load_scales(qas, qa_scales, 4)
         load_x(3)
+        load_qa(0)
         load_qa(1)
         load_qa(2)
         nc.sync.dma_start(out=cs[:], in_=cos[0].rearrange("(j p) d -> p j d", p=P))
@@ -153,14 +159,19 @@ def tile_absorbqkvo_pa_w8_kernel(
                 rhs=w.bitcast(FP8X4), rhs_scale=wsc, start=start, stop=stop,
             )
 
-        def kv_block(j):
-            n, r = bank(), bank()
-            for g in range(4):
+        kv_banks = {}
+
+        def kv_pass(j, gs):
+            if gs[0] == 0:
+                kv_banks[j] = bank(), bank()
+            n, r = kv_banks[j]
+            for g in gs:
                 a = 512 * g + 128 * j
                 mm(n[:], xc, xs, a, kvw[:, g, 256:768], kvs[4 * g : P, 256:768], g, g == 0, g == 3)
                 mm(r[:, 0:256], xc, xs, a, kvw[:, g, 0:256], kvs[4 * g : P, 0:256], g, g == 0, g == 3)
-            nc.scalar.copy(out=kvn_o[:, j, :], in_=n[:])
-            nc.scalar.copy(out=kvr_o[:, j, :], in_=r[:, 0:256])
+            if gs[-1] == 3:
+                nc.scalar.copy(out=kvn_o[:, j, :], in_=n[:])
+                nc.scalar.copy(out=kvr_o[:, j, :], in_=r[:, 0:256])
 
         def qa_tokens(j):
             t = bank()
@@ -183,16 +194,17 @@ def tile_absorbqkvo_pa_w8_kernel(
                         in_=qas[:, 512 * c : 512 * (c + 1)].rearrange("p (m t) -> p m t", t=4),
                     )
 
-        def qa_channels(c, t):
+        def qa_channels(c, ts, a, n):
             b = bank()
-            for g in range(4):
-                nc.tensor.matmul_mx(
-                    out=b[:], lhsT=qap[:, c - 1, g, 128 * t : 128 * (t + 1)].bitcast(FP8X4),
-                    lhsT_scale=qaps[4 * g : P, c - 1, 128 * t : 128 * (t + 1)],
-                    rhs=xc[:, 512 * g : 512 * (g + 1)].bitcast(FP8X4), rhs_scale=xs[:, 512 * g : 512 * (g + 1)],
-                    start=g == 0, stop=g == 3,
-                )
-            nc.scalar.copy(out=qp[:, c - 1, t, :], in_=b[:])
+            for i, t in enumerate(ts):
+                for g in range(4):
+                    nc.tensor.matmul_mx(
+                        out=b[:, n * i : n * (i + 1)], lhsT=qap[:, c - 1, g, 128 * t : 128 * (t + 1)].bitcast(FP8X4),
+                        lhsT_scale=qaps[4 * g : P, c - 1, 128 * t : 128 * (t + 1)],
+                        rhs=xc[:, 512 * g + a : 512 * g + a + n].bitcast(FP8X4), rhs_scale=xs[:, 512 * g + a : 512 * g + a + n],
+                        start=g == 0, stop=g == 3,
+                    )
+            nc.scalar.copy(out=qp[:, c - 1, ts[0] : ts[-1] + 1, a : a + n], in_=b[:].rearrange("p (t r) -> p t r", r=n))
 
         def interleave_q(c, a, n):
             nc.vector.tensor_copy(
@@ -222,21 +234,19 @@ def tile_absorbqkvo_pa_w8_kernel(
         def qb_pass(t, j, w, sc, c):
             mm(t[:], qc, qs, TOK * c + 128 * j, w[:, c], sc[4 * c : P, :], c, c == 0, c == 2)
 
-        def qb_block(j, split):
-            ws = [(qbr, qbrs[:])] + [(qbn[:, :, h, :], qbs[:, 640 * h + 128 : 640 * (h + 1)]) for h in range(HEADS)]
-            tiles = [bank() for w in ws] if split else []
-            if split:
-                for c in range(2):
-                    for t, (w, sc) in zip(tiles, ws):
-                        qb_pass(t, j, w, sc, c)
+        def rope_mm(j, cs_, t=None):
+            t = t or bank()
+            for c in cs_:
+                qb_pass(t, j, qbr, qbrs[:], c)
+            return t
 
-            def group(i):
-                t = tiles[i] if split else bank()
-                for c in range(2 if split else 0, 3):
-                    qb_pass(t, j, ws[i][0], ws[i][1], c)
-                return t
+        def nope_mm(j, h, cs_, t=None):
+            t = t or bank()
+            for c in cs_:
+                qb_pass(t, j, qbn[:, :, h, :], qbs[:, 640 * h + 128 : 640 * (h + 1)], c)
+            return t
 
-            t = group(0)
+        def rope_q(j, t):
             r3 = t[:].rearrange("p (h d) -> p h d", h=HEADS)
             ta = tmp.tile([P, HEADS, 128], F32, name="ta", tag="ta")
             tb = tmp.tile([P, HEADS, 128], F32, name="tb", tag="tb")
@@ -244,28 +254,30 @@ def tile_absorbqkvo_pa_w8_kernel(
             nc.vector.tensor_tensor(out=tb[:, :, 0:64], in0=r3[:, :, 64:128], in1=sn[:, j : j + 1, 0:64].to_broadcast([P, HEADS, 64]), op=MULT)
             nc.vector.tensor_tensor(out=tb[:, :, 64:128], in0=r3[:, :, 0:64], in1=sn[:, j : j + 1, 64:128].to_broadcast([P, HEADS, 64]), op=MULT)
             nc.vector.tensor_tensor(out=qr_o[:, j, :].rearrange("p (h d) -> p h d", h=HEADS), in0=ta[:], in1=tb[:], op=ADD)
+
+        def store_rope(j):
             nc.sync.dma_start(out=q_rope[0, :, P * j : P * (j + 1), :].rearrange("h p d -> p h d"), in_=qr_o[:, j, :].rearrange("p (h d) -> p h d", h=HEADS))
-            for h in range(HEADS):
-                if j == 3 and h == 3:
-                    halves = [bank(), bank()]
-                    for i, t in enumerate(halves):
-                        for c in range(3):
-                            mm(t[:, 0:256], qc, qs, TOK * c + 128 * j, qbn[:, c, h, 256 * i : 256 * (i + 1)],
-                               qbs[4 * c : P, 640 * h + 128 + 256 * i : 640 * h + 384 + 256 * i], c, c == 0, c == 2)
-                    for i, t in enumerate(halves):
-                        o = qn_o[:, j, h, 256 * i : 256 * (i + 1)]
-                        if i == 0:
-                            nc.vector.tensor_copy(out=o, in_=t[:, 0:256])
-                        else:
-                            nc.scalar.copy(out=o, in_=t[:, 0:256])
-                        nc.sync.dma_start(out=q_nope[0, h, P * j : P * (j + 1), 256 * i : 256 * (i + 1)], in_=o)
-                    continue
-                t = group(1 + h)
-                if h == 3:
-                    nc.vector.tensor_copy(out=qn_o[:, j, h, :], in_=t[:])
+
+        def store_nope(eng, j, h, t):
+            if eng == "v":
+                nc.vector.tensor_copy(out=qn_o[:, j, h, :], in_=t[:])
+            else:
+                nc.scalar.copy(out=qn_o[:, j, h, :], in_=t[:])
+            nc.sync.dma_start(out=q_nope[0, h, P * j : P * (j + 1), :], in_=qn_o[:, j, h, :])
+
+        def last_nope(j, h):
+            halves = [bank(), bank()]
+            for i, t in enumerate(halves):
+                for c in range(3):
+                    mm(t[:, 0:256], qc, qs, TOK * c + 128 * j, qbn[:, c, h, 256 * i : 256 * (i + 1)],
+                       qbs[4 * c : P, 640 * h + 128 + 256 * i : 640 * h + 384 + 256 * i], c, c == 0, c == 2)
+            for i, t in enumerate(halves):
+                o = qn_o[:, j, h, 256 * i : 256 * (i + 1)]
+                if i == 0:
+                    nc.vector.tensor_copy(out=o, in_=t[:, 0:256])
                 else:
-                    nc.scalar.copy(out=qn_o[:, j, h, :], in_=t[:])
-                nc.sync.dma_start(out=q_nope[0, h, P * j : P * (j + 1), :], in_=qn_o[:, j, h, :])
+                    nc.scalar.copy(out=o, in_=t[:, 0:256])
+                nc.sync.dma_start(out=q_nope[0, h, P * j : P * (j + 1), 256 * i : 256 * (i + 1)], in_=o)
 
         def rope_k():
             ra = tmp.tile([P, 4, 128], F32, name="ra", tag="ta")
@@ -276,90 +288,96 @@ def tile_absorbqkvo_pa_w8_kernel(
             nc.vector.tensor_tensor(out=kr_o[:], in0=ra[:], in1=rb[:], op=ADD)
             nc.sync.dma_start(out=k_rope[0].rearrange("(j p) d -> p j d", p=P), in_=kr_o[:])
 
-        warm_up(6)
+        warm_up(7)
         for g in range(4):
             cast_x("v" if g % 2 == 0 else "s", 0, 512 * g, 512 * (g + 1))
-        transpose_x(0)
-        warm_up(2)
+        transpose_x(0, (0,))
+        warm_up(1)
+        transpose_x(0, (1,))
+        warm_up(1)
         scale_x(0, 0)
+        for g in range(4):
+            cast_x("s", 1, 512 * g, 512 * (g + 1))
+        transpose_x(1, (0,))
         scale_x(0, 1)
         quant_x(0, 0)
         scale_x(0, 2)
         quant_x(0, 1)
         scale_x(0, 3)
         quant_x(0, 2)
-        cast_x("s", 1, 0, 1024)
-        cast_x("s", 1, 1024, 2048)
-        transpose_x(1, (0,))
-        warm_up(2)
-        transpose_x(1, (1,))
         scale_x(1, 0)
         quant_x(0, 3)
+        kv_pass(0, (0, 1))
+        transpose_x(1, (1,))
         cast_x("s", 2, 0, 1024)
         cast_x("s", 2, 1024, 2048)
-        kv_block(0)
-        scale_x(1, 1)
-        quant_x(1, 0)
-        scale_x(1, 2)
-        quant_x(1, 1)
-        scale_x(1, 3)
-        quant_x(1, 2)
+        kv_pass(0, (2, 3))
         transpose_x(2)
+        for g in range(1, 4):
+            scale_x(1, g)
+            quant_x(1, g - 1)
         scale_x(2, 0)
         quant_x(1, 3)
         cast_x("s", 3, 0, 1024)
         cast_x("s", 3, 1024, 2048)
+        kv_pass(1, (0, 1, 2, 3))
         qa_tokens(0)
-        kv_block(1)
-        scale_x(2, 1)
-        quant_x(2, 0)
-        scale_x(2, 2)
-        quant_x(2, 1)
-        scale_x(2, 3)
-        quant_x(2, 2)
-        qa_tokens(1)
+        for g in range(1, 4):
+            scale_x(2, g)
+            quant_x(2, g - 1)
         transpose_x(3)
         scale_x(3, 0)
         quant_x(2, 3)
-        scale_x(3, 1)
-        quant_x(3, 0)
-        scale_x(3, 2)
-        quant_x(3, 1)
-        scale_x(3, 3)
-        quant_x(3, 2)
+        qa_tokens(1)
+        kv_pass(2, (0, 1, 2, 3))
+        qa_tokens(2)
+        for g in range(1, 4):
+            scale_x(3, g)
+            quant_x(3, g - 1)
         permute_qa(1, (0,))
         quant_x(3, 3)
         permute_qa(1, (1, 2, 3))
-        kv_block(2)
-        qa_tokens(2)
         permute_qa(2, (0, 1, 2, 3))
-        kv_block(3)
+        kv_pass(3, (0, 1, 2, 3))
         qa_tokens(3)
         nc.vector.tensor_copy(out=qbrs[:].rearrange("p (h n) -> p h n", h=HEADS).bitcast(I32), in_=qbs[:].rearrange("p (h n) -> p h n", h=HEADS)[:, :, 0:128].bitcast(I32))
         nc.sync.dma_start(out=kv_nope[0].rearrange("(j p) d -> p j d", p=P), in_=kvn_o[:])
         nc.sync.dma_start(out=v_rope[0].rearrange("(j p) d -> p j d", p=P), in_=kvr_o[:, :, 128:256])
+        rope_k()
         for t in range(4):
-            qa_channels(1, t)
+            qa_channels(1, (t,), 0, TOK)
         ta0 = transpose_q(0)
         ta1 = transpose_q(1)
-        for t in range(4):
-            qa_channels(2, t)
+        for t in range(0, 4, 2):
+            qa_channels(2, (t, t + 1), 0, 256)
+        for t in range(0, 4, 2):
+            qa_channels(2, (t, t + 1), 256, 256)
         copy_q(0, ta0)
-        copy_q(1, ta1)
-        quant_q(0, 0, 256)
         interleave_q(1, 0, 256)
-        quant_q(0, 256, 256)
+        quant_q(0, 0, 256)
         interleave_q(1, 256, 256)
         quant_q(1, 0, 256)
+        copy_q(1, ta1)
         quant_q(1, 256, 256)
         interleave_q(2, 0, 128)
+        quant_q(0, 256, 256)
         interleave_q(2, 128, 128)
         quant_q(2, 0, 128)
-        interleave_q(2, 256, 256)
         quant_q(2, 128, 128)
+        t = rope_mm(0, (0, 1, 2))
+        rope_q(0, t)
+        interleave_q(2, 256, 256)
         quant_q(2, 256, 256)
-        qb_block(0, True)
-        rope_k()
-        qb_block(1, False)
-        qb_block(2, False)
-        qb_block(3, False)
+        for j in range(4):
+            if j < 3:
+                t = rope_mm(j + 1, (0, 1, 2))
+                rope_q(j + 1, t)
+            for h in range(HEADS):
+                if j == 3 and h == 3:
+                    last_nope(j, h)
+                else:
+                    store_nope("v" if h == 2 else "s", j, h, nope_mm(j, h, (0, 1, 2)))
+                if h == 1 and j < 3:
+                    store_rope(j)
+                if h == 3 and j == 2:
+                    store_rope(3)

@@ -30,6 +30,7 @@ def tile_absorbqkvo_pa_w8_kernel(
     with ExitStack() as ctx:
         keep = ctx.enter_context(tc.tile_pool(name="keep", bufs=1))
         tmp = ctx.enter_context(tc.tile_pool(name="tmp", bufs=2))
+        xpool = ctx.enter_context(tc.tile_pool(name="xpool", bufs=3))
         psum = ctx.enter_context(tc.psum_pool(name="psum", bufs=8))
         ctx.enter_context(tc.manual_schedule())
 
@@ -43,12 +44,10 @@ def tile_absorbqkvo_pa_w8_kernel(
         kvs = keep.tile([P, KV], U8, name="kvs", align_bytes=64)
         qaw = keep.tile([P, 3, 4, 512], U32, name="qaw", align_bytes=64)
         qas = keep.tile([P, QLR], U8, name="qas", align_bytes=64)
+        qbn = keep.tile([P, 3, HEADS, 512], U32, name="qbn", align_bytes=64)
         qbr = keep.tile([P, 3, 512], U32, name="qbr", align_bytes=64)
         qbrs = keep.tile([P, 512], U8, name="qbrs", align_bytes=64)
-        qbn = keep.tile([P, 3, 4, 512], U32, name="qbn", align_bytes=64)
         qbs = keep.tile([P, HEADS * 640], U8, name="qbs", align_bytes=64)
-        xb = keep.tile([P, 4, HID], BF16, name="xb", align_bytes=64)
-        xg = keep.tile([P, 4, HID], BF16, name="xg", align_bytes=64)
         xc = keep.tile([P, 4 * 512], U32, name="xc", align_bytes=64)
         xs = keep.tile([P, 4 * 512], U8, name="xs", align_bytes=64)
         ql = keep.tile([P, 4, 512], BF16, name="ql", align_bytes=64)
@@ -62,7 +61,7 @@ def tile_absorbqkvo_pa_w8_kernel(
         kvn_o = keep.tile([P, 4, 512], F32, name="kvn_o")
         kvr_o = keep.tile([P, 4, 256], F32, name="kvr_o")
         kr_o = keep.tile([P, 4, 128], F32, name="kr_o")
-        qr_o = keep.tile([P, 4, 512], F32, name="qr_o")
+        qr_o = keep.tile([P, 2, HEADS, 2, 128], F32, name="qr_o")
         qn_o = keep.tile([P, 4, 4, 512], F32, name="qn_o")
 
         nc.vector.memset(zero[:], 0.0)
@@ -74,8 +73,10 @@ def tile_absorbqkvo_pa_w8_kernel(
         nc.scalar.dma_start(out=xsc[:].rearrange("p (g t) -> p g t", t=4), in_=x_scale[0, 0, :].rearrange("(g p t) -> p g t", p=P, t=4))
         nc.scalar.copy(out=warm[:], in_=warm[:])
 
-        def load_x(j):
-            nc.sync.dma_start(out=xin[:, j, :], in_=x_bytes[0, P * j : P * (j + 1), :])
+        x_rows = x_bytes[0].rearrange("(q p e) k -> q p e k", q=2, e=2)
+
+        def load_x(j, a=0, n=HID):
+            nc.sync.dma_start(out=xin[:, j, a : a + n], in_=x_rows[j // 2, :, j % 2, a : a + n])
 
         def load_scales(tile, src, groups):
             for q in range(4):
@@ -84,32 +85,30 @@ def tile_absorbqkvo_pa_w8_kernel(
         def load_qa(c):
             nc.sync.dma_start(out=qaw[:, c, :, :].bitcast(I32), in_=qa_words[:, :, 512 * c : 512 * (c + 1), :].rearrange("g p n t -> p g (n t)").bitcast(I32))
 
-        def load_kv(g):
-            nc.sync.dma_start(out=kvw[:, g, :].bitcast(I32), in_=kv_words[g].rearrange("p n t -> p (n t)").bitcast(I32))
+        def load_kv(g, n):
+            nc.sync.dma_start(out=kvw[:, g : g + n, :].bitcast(I32), in_=kv_words[g : g + n].rearrange("g p n t -> p g (n t)").bitcast(I32))
 
-        for a in range(0, HID, HID // 2):
-            nc.sync.dma_start(out=xin[:, 0, a : a + HID // 2], in_=x_bytes[0, 0:P, a : a + HID // 2])
+        load_x(0, 0, HID // 2)
+        load_x(0, HID // 2, HID // 2)
         load_x(1)
         load_scales(kvs, kv_scales, 4)
-        load_kv(0)
-        load_kv(1)
+        load_kv(0, 1)
+        load_kv(1, 1)
         load_x(2)
-        load_kv(2)
-        load_kv(3)
-        load_scales(qas, qa_scales, 4)
+        load_kv(2, 1)
+        load_kv(3, 1)
         load_x(3)
+        load_scales(qas, qa_scales, 4)
         load_qa(0)
         load_qa(1)
         load_qa(2)
-        nc.sync.dma_start(out=cs[:], in_=cos[0].rearrange("(j p) d -> p j d", p=P))
-        nc.sync.dma_start(out=sn[:], in_=sin[0].rearrange("(j p) d -> p j d", p=P))
+        for tile, src in ((cs, cos), (sn, sin)):
+            nc.sync.dma_start(out=tile[:].rearrange("p (q e) d -> p q (e d)", q=2), in_=src[0].rearrange("(q p e) d -> p q (e d)", q=2, e=2))
         load_scales(qbs, qb_scales, 3)
         for g in range(3):
-            wg = qb_words[g].rearrange("p (h n) t -> p h n t", h=HEADS)
-            nc.sync.dma_start(out=qbr[:, g, :].rearrange("p (h n) -> p h n", h=HEADS).bitcast(I32), in_=wg[:, :, 0:128, :].rearrange("p h n t -> p h (n t)").bitcast(I32))
-        for g in range(3):
-            wg = qb_words[g].rearrange("p (h n) t -> p h n t", h=HEADS)
-            nc.sync.dma_start(out=qbn[:, g, :, :].bitcast(I32), in_=wg[:, :, 128:640, :].rearrange("p h n t -> p h (n t)").bitcast(I32))
+            w = qb_words[g].rearrange("p (h n) t -> p h (n t)", h=HEADS)
+            nc.sync.dma_start(out=qbr[:, g, :].rearrange("p (h n) -> p h n", h=HEADS).bitcast(I32), in_=w[:, :, 0:512].bitcast(I32))
+            nc.sync.dma_start(out=qbn[:, g, :, :].bitcast(I32), in_=w[:, :, 512:2560].bitcast(I32))
         nc.gpsimd.tensor_scalar(out=sn[:, :, 0:64], in0=sn[:, :, 0:64], scalar1=-1.0, scalar2=0.0, op0=MULT, op1=ADD)
 
         def bank():
@@ -121,8 +120,11 @@ def tile_absorbqkvo_pa_w8_kernel(
             for i in range(n):
                 nc.tensor.matmul(dummy[:], lhsT=zero[:, 0:128], rhs=zero[:], start=True, stop=True)
 
+        xb = [xpool.tile([P, HID], BF16, name="xb%d" % j, tag="xb", align_bytes=64) for j in range(4)]
+        xg = [xpool.tile([P, HID], BF16, name="xg%d" % j, tag="xg", align_bytes=64) for j in range(4)]
+
         def cast_x(eng, j, a, b):
-            dst, src = xb[:, j, a:b], xin[:, j, a:b].bitcast(FP8)
+            dst, src = xb[j][:, a:b], xin[:, j, a:b].bitcast(FP8)
             if eng == "v":
                 nc.vector.tensor_copy(out=dst, in_=src)
             else:
@@ -131,7 +133,7 @@ def tile_absorbqkvo_pa_w8_kernel(
         xt = {}
 
         def transpose_x(j, halves=(0, 1)):
-            words = xb[:, j, :].bitcast(F32)
+            words = xb[j][:].bitcast(F32)
             for half in halves:
                 t = bank()
                 for gg in range(2):
@@ -143,7 +145,7 @@ def tile_absorbqkvo_pa_w8_kernel(
 
         def scale_x(j, g):
             nc.vector.tensor_tensor(
-                out=xg[:, j, 512 * g : 512 * (g + 1)].rearrange("p (r u e) -> p r u e", u=2, e=2),
+                out=xg[j][:, 512 * g : 512 * (g + 1)].rearrange("p (r u e) -> p r u e", u=2, e=2),
                 in0=xt[j, g].bitcast(BF16).rearrange("p (u r e) -> p r u e", u=2, e=2),
                 in1=xsc[:, 4 * g : 4 * g + 4].rearrange("p (o u e) -> p o u e", o=1, u=2).to_broadcast([P, P, 2, 2]),
                 op=MULT,
@@ -151,7 +153,7 @@ def tile_absorbqkvo_pa_w8_kernel(
 
         def quant_x(j, g):
             a = 512 * g + 128 * j
-            nc.vector.quantize_mx(out=xc[:, a : a + 128].bitcast(FP8X4), scales=xs[:, a : a + 128], in_=xg[:, j, 512 * g : 512 * (g + 1)])
+            nc.vector.quantize_mx(out=xc[:, a : a + 128].bitcast(FP8X4), scales=xs[:, a : a + 128], in_=xg[j][:, 512 * g : 512 * (g + 1)])
 
         def mm(out, codes, scales, a, w, wsc, g, start, stop):
             nc.tensor.matmul_mx(
@@ -253,17 +255,21 @@ def tile_absorbqkvo_pa_w8_kernel(
             nc.vector.tensor_tensor(out=ta[:], in0=r3, in1=cs[:, j : j + 1, :].to_broadcast([P, HEADS, 128]), op=MULT)
             nc.vector.tensor_tensor(out=tb[:, :, 0:64], in0=r3[:, :, 64:128], in1=sn[:, j : j + 1, 0:64].to_broadcast([P, HEADS, 64]), op=MULT)
             nc.vector.tensor_tensor(out=tb[:, :, 64:128], in0=r3[:, :, 0:64], in1=sn[:, j : j + 1, 64:128].to_broadcast([P, HEADS, 64]), op=MULT)
-            nc.vector.tensor_tensor(out=qr_o[:, j, :].rearrange("p (h d) -> p h d", h=HEADS), in0=ta[:], in1=tb[:], op=ADD)
+            nc.vector.tensor_tensor(out=qr_o[:, j // 2, :, j % 2, :], in0=ta[:], in1=tb[:], op=ADD)
 
-        def store_rope(j):
-            nc.sync.dma_start(out=q_rope[0, :, P * j : P * (j + 1), :].rearrange("h p d -> p h d"), in_=qr_o[:, j, :].rearrange("p (h d) -> p h d", h=HEADS))
+        def store_rope(q):
+            nc.sync.dma_start(out=q_rope[0, :, 256 * q : 256 * (q + 1), :].rearrange("h (p e) d -> p h (e d)", e=2), in_=qr_o[:, q, :, :, :].rearrange("p h e d -> p h (e d)"))
 
-        def store_nope(eng, j, h, t):
+        nope_rows = q_nope[0].rearrange("h (q p e) d -> q e p h d", q=2, e=2)
+
+        def copy_nope(eng, j, h, t):
             if eng == "v":
                 nc.vector.tensor_copy(out=qn_o[:, j, h, :], in_=t[:])
             else:
                 nc.scalar.copy(out=qn_o[:, j, h, :], in_=t[:])
-            nc.sync.dma_start(out=q_nope[0, h, P * j : P * (j + 1), :], in_=qn_o[:, j, h, :])
+
+        def store_nope(j, h, n):
+            nc.sync.dma_start(out=nope_rows[j // 2, j % 2, :, h : h + n, :], in_=qn_o[:, j, h : h + n, :])
 
         def last_nope(j, h):
             halves = [bank(), bank()]
@@ -277,7 +283,7 @@ def tile_absorbqkvo_pa_w8_kernel(
                     nc.vector.tensor_copy(out=o, in_=t[:, 0:256])
                 else:
                     nc.scalar.copy(out=o, in_=t[:, 0:256])
-                nc.sync.dma_start(out=q_nope[0, h, P * j : P * (j + 1), 256 * i : 256 * (i + 1)], in_=o)
+                nc.sync.dma_start(out=nope_rows[j // 2, j % 2, :, h, 256 * i : 256 * (i + 1)], in_=o)
 
         def rope_k():
             ra = tmp.tile([P, 4, 128], F32, name="ra", tag="ta")
@@ -286,7 +292,7 @@ def tile_absorbqkvo_pa_w8_kernel(
             nc.vector.tensor_tensor(out=rb[:, :, 0:64], in0=kvr_o[:, :, 64:128], in1=sn[:, :, 0:64], op=MULT)
             nc.vector.tensor_tensor(out=rb[:, :, 64:128], in0=kvr_o[:, :, 0:64], in1=sn[:, :, 64:128], op=MULT)
             nc.vector.tensor_tensor(out=kr_o[:], in0=ra[:], in1=rb[:], op=ADD)
-            nc.sync.dma_start(out=k_rope[0].rearrange("(j p) d -> p j d", p=P), in_=kr_o[:])
+            nc.sync.dma_start(out=k_rope[0].rearrange("(q p e) d -> p q (e d)", q=2, e=2), in_=kr_o[:].rearrange("p (q e) d -> p q (e d)", q=2))
 
         warm_up(7)
         for g in range(4):
@@ -321,11 +327,11 @@ def tile_absorbqkvo_pa_w8_kernel(
         cast_x("s", 3, 0, 1024)
         cast_x("s", 3, 1024, 2048)
         kv_pass(1, (0, 1, 2, 3))
+        transpose_x(3)
         qa_tokens(0)
         for g in range(1, 4):
             scale_x(2, g)
             quant_x(2, g - 1)
-        transpose_x(3)
         scale_x(3, 0)
         quant_x(2, 3)
         qa_tokens(1)
@@ -341,8 +347,9 @@ def tile_absorbqkvo_pa_w8_kernel(
         kv_pass(3, (0, 1, 2, 3))
         qa_tokens(3)
         nc.vector.tensor_copy(out=qbrs[:].rearrange("p (h n) -> p h n", h=HEADS).bitcast(I32), in_=qbs[:].rearrange("p (h n) -> p h n", h=HEADS)[:, :, 0:128].bitcast(I32))
-        nc.sync.dma_start(out=kv_nope[0].rearrange("(j p) d -> p j d", p=P), in_=kvn_o[:])
-        nc.sync.dma_start(out=v_rope[0].rearrange("(j p) d -> p j d", p=P), in_=kvr_o[:, :, 128:256])
+        nc.sync.dma_start(out=kv_nope[0].rearrange("(q p e) d -> p q (e d)", q=2, e=2), in_=kvn_o[:].rearrange("p (q e) d -> p q (e d)", q=2))
+        for q in range(2):
+            nc.sync.dma_start(out=v_rope[0, 256 * q : 256 * (q + 1), :].rearrange("(p e) d -> p e d", e=2), in_=kvr_o[:, 2 * q : 2 * q + 2, 128:256])
         rope_k()
         for t in range(4):
             qa_channels(1, (t,), 0, TOK)
@@ -375,9 +382,11 @@ def tile_absorbqkvo_pa_w8_kernel(
             for h in range(HEADS):
                 if j == 3 and h == 3:
                     last_nope(j, h)
-                else:
-                    store_nope("v" if h == 2 else "s", j, h, nope_mm(j, h, (0, 1, 2)))
-                if h == 1 and j < 3:
-                    store_rope(j)
-                if h == 3 and j == 2:
-                    store_rope(3)
+                    break
+                copy_nope("v" if h == 2 else "s", j, h, nope_mm(j, h, (0, 1, 2)))
+                if h == 1 or (j == 3 and h == 2):
+                    store_nope(j, 2 * (h // 2), 1 + h % 2)
+                if h == 1 and j in (0, 2):
+                    store_rope(j // 2)
+                if h == 3:
+                    store_nope(j, 2, 2)

@@ -64,9 +64,9 @@ def tile_absorbqkvo_pa_w8_kernel(
         qr_o = keep.tile([P, 2, HEADS, 2, 128], F32, name="qr_o")
         qn_o = keep.tile([P, 4, 4, 512], F32, name="qn_o")
 
+        nc.vector.memset(kvs[:].bitcast(I32), 0)
         nc.vector.memset(zero[:], 0.0)
         nc.vector.memset(warm[:], 0.0)
-        nc.vector.memset(kvs[:].bitcast(I32), 0)
         nc.vector.memset(qas[:].bitcast(I32), 0)
         nc.vector.memset(qbs[:].bitcast(I32), 0)
         make_identity(nc, ident[:])
@@ -90,8 +90,8 @@ def tile_absorbqkvo_pa_w8_kernel(
 
         load_x(0, 0, HID // 2)
         load_x(0, HID // 2, HID // 2)
-        load_x(1)
         load_scales(kvs, kv_scales, 4)
+        load_x(1)
         load_kv(0, 1)
         load_kv(1, 1)
         load_x(2)
@@ -351,42 +351,58 @@ def tile_absorbqkvo_pa_w8_kernel(
         for q in range(2):
             nc.sync.dma_start(out=v_rope[0, 256 * q : 256 * (q + 1), :].rearrange("(p e) d -> p e d", e=2), in_=kvr_o[:, 2 * q : 2 * q + 2, 128:256])
         rope_k()
-        for t in range(4):
-            qa_channels(1, (t,), 0, TOK)
+        for t in (0, 2):
+            qa_channels(1, (t, t + 1), 0, 256)
         ta0 = transpose_q(0)
         ta1 = transpose_q(1)
-        for t in range(0, 4, 2):
+        for t in (0, 2):
             qa_channels(2, (t, t + 1), 0, 256)
-        for t in range(0, 4, 2):
-            qa_channels(2, (t, t + 1), 256, 256)
+        for t in (0, 2):
+            qa_channels(1, (t, t + 1), 256, 256)
         copy_q(0, ta0)
         interleave_q(1, 0, 256)
         quant_q(0, 0, 256)
-        interleave_q(1, 256, 256)
-        quant_q(1, 0, 256)
         copy_q(1, ta1)
-        quant_q(1, 256, 256)
-        interleave_q(2, 0, 128)
+        quant_q(1, 0, 256)
         quant_q(0, 256, 256)
+        interleave_q(2, 0, 128)
         interleave_q(2, 128, 128)
         quant_q(2, 0, 128)
         quant_q(2, 128, 128)
-        t = rope_mm(0, (0, 1, 2))
-        rope_q(0, t)
-        interleave_q(2, 256, 256)
-        quant_q(2, 256, 256)
-        for j in range(4):
-            if j < 3:
-                t = rope_mm(j + 1, (0, 1, 2))
-                rope_q(j + 1, t)
-            for h in range(HEADS):
-                if j == 3 and h == 3:
-                    last_nope(j, h)
-                    break
-                copy_nope("v" if h == 2 else "s", j, h, nope_mm(j, h, (0, 1, 2)))
-                if h == 1 or (j == 3 and h == 2):
-                    store_nope(j, 2 * (h // 2), 1 + h % 2)
-                if h == 1 and j in (0, 2):
-                    store_rope(j // 2)
-                if h == 3:
-                    store_nope(j, 2, 2)
+        rope_q(0, rope_mm(0, (0, 1, 2)))
+        interleave_q(1, 256, 256)
+        rope_q(1, rope_mm(1, (0, 1, 2)))
+        quant_q(1, 256, 256)
+
+        def nope(j, h):
+            if j == 3 and h == 3:
+                last_nope(j, h)
+                return
+            copy_nope("v" if h == 2 else "s", j, h, nope_mm(j, h, (0, 1, 2)))
+            if h == 1 or (j == 3 and h == 2):
+                store_nope(j, 2 * (h // 2), 1 + h % 2)
+            elif h == 3:
+                store_nope(j, 2, 2)
+
+        for h in range(HEADS):
+            nope(0, h)
+        store_rope(0)
+        for t in (0, 2):
+            qa_channels(2, (t, t + 1), 256, 256)
+        nope(1, 0)
+        nope(1, 1)
+        interleave_q(2, 256, 128)
+        interleave_q(2, 384, 128)
+        quant_q(2, 256, 128)
+        quant_q(2, 384, 128)
+        nope(1, 2)
+        rope_q(2, rope_mm(2, (0, 1, 2)))
+        nope(1, 3)
+        rope_q(3, rope_mm(3, (0, 1, 2)))
+        nope(2, 0)
+        nope(2, 1)
+        store_rope(1)
+        nope(2, 2)
+        nope(2, 3)
+        for h in range(HEADS):
+            nope(3, h)

@@ -70,7 +70,6 @@ def tile_absorbqkvo_pa_w8_kernel(
         nc.vector.memset(qas[:].bitcast(I32), 0)
         nc.vector.memset(qbs[:].bitcast(I32), 0)
         make_identity(nc, ident[:])
-        nc.scalar.dma_start(out=xsc[:].rearrange("p (g t) -> p g t", t=4), in_=x_scale[0, 0, :].rearrange("(g p t) -> p g t", p=P, t=4))
         nc.scalar.copy(out=warm[:], in_=warm[:])
 
         x_rows = x_bytes[0].rearrange("(q p e) k -> q p e k", q=2, e=2)
@@ -90,6 +89,7 @@ def tile_absorbqkvo_pa_w8_kernel(
 
         load_x(0, 0, HID // 2)
         load_x(0, HID // 2, HID // 2)
+        nc.sync.dma_start(out=xsc[:].rearrange("p (g t) -> p g t", t=4), in_=x_scale[0, 0, :].rearrange("(g p t) -> p g t", p=P, t=4))
         load_scales(kvs, kv_scales, 4)
         load_x(1)
         load_kv(0, 1)
@@ -163,17 +163,41 @@ def tile_absorbqkvo_pa_w8_kernel(
 
         kv_banks = {}
 
-        def kv_pass(j, gs):
+        def kv_pass(j, gs, nope):
             if gs[0] == 0:
-                kv_banks[j] = bank(), bank()
-            n, r = kv_banks[j]
+                kv_banks[j] = bank(), (bank() if nope else None)
+            r, n = kv_banks[j]
             for g in gs:
                 a = 512 * g + 128 * j
-                mm(n[:], xc, xs, a, kvw[:, g, 256:768], kvs[4 * g : P, 256:768], g, g == 0, g == 3)
+                if nope:
+                    mm(n[:], xc, xs, a, kvw[:, g, 256:768], kvs[4 * g : P, 256:768], g, g == 0, g == 3)
                 mm(r[:, 0:256], xc, xs, a, kvw[:, g, 0:256], kvs[4 * g : P, 0:256], g, g == 0, g == 3)
             if gs[-1] == 3:
-                nc.scalar.copy(out=kvn_o[:, j, :], in_=n[:])
+                if nope:
+                    nc.scalar.copy(out=kvn_o[:, j, :], in_=n[:])
                 nc.scalar.copy(out=kvr_o[:, j, :], in_=r[:, 0:256])
+
+        kvn_rows = kv_nope[0].rearrange("(q p e) d -> p q e d", q=2, e=2)
+
+        def kv_nope_late(j):
+            if j == 2:
+                t = bank()
+                for g in range(4):
+                    mm(t[:], xc, xs, 512 * g + 128 * j, kvw[:, g, 256:768], kvs[4 * g : P, 256:768], g, g == 0, g == 3)
+                nc.scalar.copy(out=kvn_o[:, j, :], in_=t[:])
+                nc.sync.dma_start(out=kvn_rows[:, 1, 0, :], in_=kvn_o[:, j, :])
+                return
+            halves = [bank(), bank()]
+            for i, t in enumerate(halves):
+                a = 256 + 256 * i
+                for g in range(4):
+                    mm(t[:, 0:256], xc, xs, 512 * g + 128 * j, kvw[:, g, a : a + 256], kvs[4 * g : P, a : a + 256], g, g == 0, g == 3)
+                o = kvn_o[:, j, 256 * i : 256 * (i + 1)]
+                if i == 0:
+                    nc.vector.tensor_copy(out=o, in_=t[:, 0:256])
+                else:
+                    nc.scalar.copy(out=o, in_=t[:, 0:256])
+                nc.sync.dma_start(out=kvn_rows[:, 1, 1, 256 * i : 256 * (i + 1)], in_=o)
 
         def qa_tokens(j):
             t = bank()
@@ -271,20 +295,6 @@ def tile_absorbqkvo_pa_w8_kernel(
         def store_nope(j, h, n):
             nc.sync.dma_start(out=nope_rows[j // 2, j % 2, :, h : h + n, :], in_=qn_o[:, j, h : h + n, :])
 
-        def last_nope(j, h):
-            halves = [bank(), bank()]
-            for i, t in enumerate(halves):
-                for c in range(3):
-                    mm(t[:, 0:256], qc, qs, TOK * c + 128 * j, qbn[:, c, h, 256 * i : 256 * (i + 1)],
-                       qbs[4 * c : P, 640 * h + 128 + 256 * i : 640 * h + 384 + 256 * i], c, c == 0, c == 2)
-            for i, t in enumerate(halves):
-                o = qn_o[:, j, h, 256 * i : 256 * (i + 1)]
-                if i == 0:
-                    nc.vector.tensor_copy(out=o, in_=t[:, 0:256])
-                else:
-                    nc.scalar.copy(out=o, in_=t[:, 0:256])
-                nc.sync.dma_start(out=nope_rows[j // 2, j % 2, :, h, 256 * i : 256 * (i + 1)], in_=o)
-
         def rope_k():
             ra = tmp.tile([P, 4, 128], F32, name="ra", tag="ta")
             rb = tmp.tile([P, 4, 128], F32, name="rb", tag="tb")
@@ -313,11 +323,11 @@ def tile_absorbqkvo_pa_w8_kernel(
         quant_x(0, 2)
         scale_x(1, 0)
         quant_x(0, 3)
-        kv_pass(0, (0, 1))
+        kv_pass(0, (0, 1), True)
         transpose_x(1, (1,))
         cast_x("s", 2, 0, 1024)
         cast_x("s", 2, 1024, 2048)
-        kv_pass(0, (2, 3))
+        kv_pass(0, (2, 3), True)
         transpose_x(2)
         for g in range(1, 4):
             scale_x(1, g)
@@ -326,7 +336,7 @@ def tile_absorbqkvo_pa_w8_kernel(
         quant_x(1, 3)
         cast_x("s", 3, 0, 1024)
         cast_x("s", 3, 1024, 2048)
-        kv_pass(1, (0, 1, 2, 3))
+        kv_pass(1, (0, 1, 2, 3), True)
         transpose_x(3)
         qa_tokens(0)
         for g in range(1, 4):
@@ -335,7 +345,7 @@ def tile_absorbqkvo_pa_w8_kernel(
         scale_x(3, 0)
         quant_x(2, 3)
         qa_tokens(1)
-        kv_pass(2, (0, 1, 2, 3))
+        kv_pass(2, (0, 1, 2, 3), False)
         qa_tokens(2)
         for g in range(1, 4):
             scale_x(3, g)
@@ -344,10 +354,10 @@ def tile_absorbqkvo_pa_w8_kernel(
         quant_x(3, 3)
         permute_qa(1, (1, 2, 3))
         permute_qa(2, (0, 1, 2, 3))
-        kv_pass(3, (0, 1, 2, 3))
+        kv_pass(3, (0, 1, 2, 3), False)
         qa_tokens(3)
         nc.vector.tensor_copy(out=qbrs[:].rearrange("p (h n) -> p h n", h=HEADS).bitcast(I32), in_=qbs[:].rearrange("p (h n) -> p h n", h=HEADS)[:, :, 0:128].bitcast(I32))
-        nc.sync.dma_start(out=kv_nope[0].rearrange("(q p e) d -> p q (e d)", q=2, e=2), in_=kvn_o[:].rearrange("p (q e) d -> p q (e d)", q=2))
+        nc.sync.dma_start(out=kvn_rows[:, 0, :, :], in_=kvn_o[:, 0:2, :])
         for q in range(2):
             nc.sync.dma_start(out=v_rope[0, 256 * q : 256 * (q + 1), :].rearrange("(p e) d -> p e d", e=2), in_=kvr_o[:, 2 * q : 2 * q + 2, 128:256])
         rope_k()
@@ -375,14 +385,9 @@ def tile_absorbqkvo_pa_w8_kernel(
         quant_q(1, 256, 256)
 
         def nope(j, h):
-            if j == 3 and h == 3:
-                last_nope(j, h)
-                return
             copy_nope("v" if h == 2 else "s", j, h, nope_mm(j, h, (0, 1, 2)))
-            if h == 1 or (j == 3 and h == 2):
-                store_nope(j, 2 * (h // 2), 1 + h % 2)
-            elif h == 3:
-                store_nope(j, 2, 2)
+            if h % 2:
+                store_nope(j, h - 1, 2)
 
         for h in range(HEADS):
             nope(0, h)
@@ -406,3 +411,5 @@ def tile_absorbqkvo_pa_w8_kernel(
         nope(2, 3)
         for h in range(HEADS):
             nope(3, h)
+        kv_nope_late(2)
+        kv_nope_late(3)

from contextlib import ExitStack

import concourse.mybir as mybir
from concourse.masks import make_identity

F32 = mybir.dt.float32
BF16 = mybir.dt.bfloat16
U32 = mybir.dt.uint32
I32 = mybir.dt.int32
U8 = mybir.dt.uint8
FP8 = mybir.dt.float8_e4m3fn
FP8X4 = mybir.dt.float8_e4m3fn_x4
MULT = mybir.AluOpType.mult
ADD = mybir.AluOpType.add

P = 128
TOK = 512
HID = 2048
QLR = 1536
HEADS = 4
KV = 768
FLOPS = 2 * TOK * (HID * QLR + QLR * HEADS * 640 + HID * KV)


def tile_absorbqkvo_pa_w8_kernel(
    tc, x_bytes, x_scale, cos, sin, qa_words, qa_scales, qb_words, qb_scales, kv_words, kv_scales,
    q_rope, q_nope, k_rope, v_rope, kv_nope,
):
    nc = tc.nc
    with ExitStack() as ctx:
        keep = ctx.enter_context(tc.tile_pool(name="keep", bufs=1))
        tmp = ctx.enter_context(tc.tile_pool(name="tmp", bufs=2))
        xpool = ctx.enter_context(tc.tile_pool(name="xpool", bufs=3))
        psum = ctx.enter_context(tc.psum_pool(name="psum", bufs=8))
        ctx.enter_context(tc.manual_schedule())

        ident = keep.tile([P, P], F32, name="ident")
        warm = keep.tile([P, 1], F32, name="warm")
        xin = keep.tile([P, 4, HID], U8, name="xin", align_bytes=64)
        xsc = keep.tile([P, 16], F32, name="xsc")
        cs = keep.tile([P, 4, 128], BF16, name="cs", align_bytes=64)
        sn = keep.tile([P, 4, 128], BF16, name="sn", align_bytes=64)
        kvw = keep.tile([P, 4, KV], U32, name="kvw", align_bytes=64)
        kvs = keep.tile([P, KV], U8, name="kvs", align_bytes=64)
        qaw = keep.tile([P, 3, 4, 512], U32, name="qaw", align_bytes=64)
        qas = keep.tile([P, QLR], U8, name="qas", align_bytes=64)
        qbn = keep.tile([P, 3, HEADS, 512], U32, name="qbn", align_bytes=64)
        qbr = keep.tile([P, 3, 512], U32, name="qbr", align_bytes=64)
        qbrs = keep.tile([P, 512], U8, name="qbrs", align_bytes=64)
        qbs = keep.tile([P, HEADS * 640], U8, name="qbs", align_bytes=64)
        xc = keep.tile([P, 4 * 512], U32, name="xc", align_bytes=64)
        xs = keep.tile([P, 4 * 512], U8, name="xs", align_bytes=64)
        ql = keep.tile([P, 4, 512], BF16, name="ql", align_bytes=64)
        qp = keep.tile([P, 2, 4, TOK], BF16, name="qp", align_bytes=64)
        qg = keep.tile([P, 3, TOK * 4], BF16, name="qg", align_bytes=64)
        qc = keep.tile([P, 3 * TOK], U32, name="qc", align_bytes=64)
        qs = keep.tile([P, 3 * TOK], U8, name="qs", align_bytes=64)
        qap = keep.tile([P, 2, 4, 512], U32, name="qap", align_bytes=64)
        qaps = keep.tile([P, 2, 512], U8, name="qaps", align_bytes=64)
        zero = keep.tile([P, 512], BF16, name="zero")
        kvn_o = keep.tile([P, 4, 512], F32, name="kvn_o")
        kvr_o = keep.tile([P, 4, 256], F32, name="kvr_o")
        kr_o = keep.tile([P, 4, 128], F32, name="kr_o")
        qr_o = keep.tile([P, 2, HEADS, 2, 128], F32, name="qr_o")
        qn_o = keep.tile([P, 4, 4, 512], F32, name="qn_o")

        nc.vector.memset(kvs[:].bitcast(I32), 0)
        nc.vector.memset(zero[:], 0.0)
        nc.vector.memset(warm[:], 0.0)
        nc.vector.memset(qas[:].bitcast(I32), 0)
        nc.vector.memset(qbs[:].bitcast(I32), 0)
        make_identity(nc, ident[:])
        nc.scalar.copy(out=warm[:], in_=warm[:])

        x_rows = x_bytes[0].rearrange("(q p e) k -> q p e k", q=2, e=2)

        def load_x(j, a=0, n=HID):
            nc.sync.dma_start(out=xin[:, j, a : a + n], in_=x_rows[j // 2, :, j % 2, a : a + n])

        def load_scales(tile, src, groups):
            for q in range(4):
                nc.sync.dma_start(out=tile[32 * q : 32 * q + 4 * groups, :].bitcast(I32), in_=src[:, 4 * q : 4 * q + 4, :].bitcast(I32))

        def load_qa(c):
            nc.sync.dma_start(out=qaw[:, c, :, :].bitcast(I32), in_=qa_words[:, :, 512 * c : 512 * (c + 1), :].rearrange("g p n t -> p g (n t)").bitcast(I32))

        def load_kv(g, n):
            nc.sync.dma_start(out=kvw[:, g : g + n, :].bitcast(I32), in_=kv_words[g : g + n].rearrange("g p n t -> p g (n t)").bitcast(I32))

        load_x(0, 0, HID // 2)
        load_x(0, HID // 2, HID // 2)
        nc.sync.dma_start(out=xsc[:].rearrange("p (g t) -> p g t", t=4), in_=x_scale[0, 0, :].rearrange("(g p t) -> p g t", p=P, t=4))
        load_scales(kvs, kv_scales, 4)
        load_x(1)
        load_kv(0, 1)
        load_kv(1, 1)
        load_x(2)
        load_kv(2, 1)
        load_kv(3, 1)
        load_x(3)
        load_scales(qas, qa_scales, 4)
        load_qa(0)
        load_qa(1)
        load_qa(2)
        for tile, src in ((cs, cos), (sn, sin)):
            nc.sync.dma_start(out=tile[:].rearrange("p (q e) d -> p q (e d)", q=2), in_=src[0].rearrange("(q p e) d -> p q (e d)", q=2, e=2))
        load_scales(qbs, qb_scales, 3)
        for g in range(3):
            w = qb_words[g].rearrange("p (h n) t -> p h (n t)", h=HEADS)
            nc.sync.dma_start(out=qbr[:, g, :].rearrange("p (h n) -> p h n", h=HEADS).bitcast(I32), in_=w[:, :, 0:512].bitcast(I32))
            nc.sync.dma_start(out=qbn[:, g, :, :].bitcast(I32), in_=w[:, :, 512:2560].bitcast(I32))
        nc.gpsimd.tensor_scalar(out=sn[:, :, 0:64], in0=sn[:, :, 0:64], scalar1=-1.0, scalar2=0.0, op0=MULT, op1=ADD)

        def bank():
            return psum.tile([P, 512], F32, name="bank", tag="bank")

        dummy = bank()

        def warm_up(n):
            for i in range(n):
                nc.tensor.matmul(dummy[:], lhsT=zero[:, 0:128], rhs=zero[:], start=True, stop=True)

        xb = [xpool.tile([P, HID], BF16, name="xb%d" % j, tag="xb", align_bytes=64) for j in range(4)]
        xg = [xpool.tile([P, HID], BF16, name="xg%d" % j, tag="xg", align_bytes=64) for j in range(4)]

        def cast_x(eng, j, a, b):
            dst, src = xb[j][:, a:b], xin[:, j, a:b].bitcast(FP8)
            if eng == "v":
                nc.vector.tensor_copy(out=dst, in_=src)
            else:
                nc.scalar.copy(out=dst, in_=src)

        xt = {}

        def transpose_x(j, halves=(0, 1)):
            words = xb[j][:].bitcast(F32)
            for half in halves:
                t = bank()
                for gg in range(2):
                    g = 2 * half + gg
                    for u in range(2):
                        o = 256 * gg + 128 * u
                        nc.tensor.transpose(t[:, o : o + 128], words[:, 256 * g + u : 256 * (g + 1) : 2], ident[:])
                    xt[j, g] = t[:, 256 * gg : 256 * (gg + 1)]

        def scale_x(j, g):
            nc.vector.tensor_tensor(
                out=xg[j][:, 512 * g : 512 * (g + 1)].rearrange("p (r u e) -> p r u e", u=2, e=2),
                in0=xt[j, g].bitcast(BF16).rearrange("p (u r e) -> p r u e", u=2, e=2),
                in1=xsc[:, 4 * g : 4 * g + 4].rearrange("p (o u e) -> p o u e", o=1, u=2).to_broadcast([P, P, 2, 2]),
                op=MULT,
            )

        def quant_x(j, g):
            a = 512 * g + 128 * j
            nc.vector.quantize_mx(out=xc[:, a : a + 128].bitcast(FP8X4), scales=xs[:, a : a + 128], in_=xg[j][:, 512 * g : 512 * (g + 1)])

        def mm(out, codes, scales, a, w, wsc, g, start, stop):
            nc.tensor.matmul_mx(
                out=out, lhsT=codes[:, a : a + 128].bitcast(FP8X4), lhsT_scale=scales[:, a : a + 128],
                rhs=w.bitcast(FP8X4), rhs_scale=wsc, start=start, stop=stop,
            )

        kv_banks = {}

        def kv_pass(j, gs, nope):
            if gs[0] == 0:
                kv_banks[j] = bank(), (bank() if nope else None)
            r, n = kv_banks[j]
            for g in gs:
                a = 512 * g + 128 * j
                if nope:
                    mm(n[:], xc, xs, a, kvw[:, g, 256:768], kvs[4 * g : P, 256:768], g, g == 0, g == 3)
                mm(r[:, 0:256], xc, xs, a, kvw[:, g, 0:256], kvs[4 * g : P, 0:256], g, g == 0, g == 3)
            if gs[-1] == 3:
                if nope:
                    nc.scalar.copy(out=kvn_o[:, j, :], in_=n[:])
                nc.scalar.copy(out=kvr_o[:, j, :], in_=r[:, 0:256])

        kvn_rows = kv_nope[0].rearrange("(q p e) d -> p q e d", q=2, e=2)

        def kv_nope_late(j):
            if j == 2:
                t = bank()
                for g in range(4):
                    mm(t[:], xc, xs, 512 * g + 128 * j, kvw[:, g, 256:768], kvs[4 * g : P, 256:768], g, g == 0, g == 3)
                nc.scalar.copy(out=kvn_o[:, j, :], in_=t[:])
                nc.sync.dma_start(out=kvn_rows[:, 1, 0, :], in_=kvn_o[:, j, :])
                return
            halves = [bank(), bank()]
            for i, t in enumerate(halves):
                a = 256 + 256 * i
                for g in range(4):
                    mm(t[:, 0:256], xc, xs, 512 * g + 128 * j, kvw[:, g, a : a + 256], kvs[4 * g : P, a : a + 256], g, g == 0, g == 3)
                o = kvn_o[:, j, 256 * i : 256 * (i + 1)]
                if i == 0:
                    nc.vector.tensor_copy(out=o, in_=t[:, 0:256])
                else:
                    nc.scalar.copy(out=o, in_=t[:, 0:256])
                nc.sync.dma_start(out=kvn_rows[:, 1, 1, 256 * i : 256 * (i + 1)], in_=o)

        def qa_tokens(j):
            t = bank()
            for g in range(4):
                mm(t[:], xc, xs, 512 * g + 128 * j, qaw[:, 0, g, :], qas[4 * g : P, 0:512], g, g == 0, g == 3)
            nc.scalar.copy(
                out=ql[:, j, :].rearrange("p (u w e) -> p u w e", u=2, e=2),
                in_=t[:].rearrange("p (w u e) -> p u w e", u=2, e=2),
            )

        def permute_qa(c, ts):
            for t in ts:
                nc.vector.tensor_copy(
                    out=qap[:, c - 1, :, 128 * t : 128 * (t + 1)].bitcast(I32),
                    in_=qaw[:, c, :, t:512:4].bitcast(I32),
                )
                if t == 0:
                    nc.vector.tensor_copy(
                        out=qaps[:, c - 1, :].rearrange("p (t m) -> p m t", t=4),
                        in_=qas[:, 512 * c : 512 * (c + 1)].rearrange("p (m t) -> p m t", t=4),
                    )

        def qa_channels(c, ts, a, n):
            b = bank()
            for i, t in enumerate(ts):
                for g in range(4):
                    nc.tensor.matmul_mx(
                        out=b[:, n * i : n * (i + 1)], lhsT=qap[:, c - 1, g, 128 * t : 128 * (t + 1)].bitcast(FP8X4),
                        lhsT_scale=qaps[4 * g : P, c - 1, 128 * t : 128 * (t + 1)],
                        rhs=xc[:, 512 * g + a : 512 * g + a + n].bitcast(FP8X4), rhs_scale=xs[:, 512 * g + a : 512 * g + a + n],
                        start=g == 0, stop=g == 3,
                    )
            nc.scalar.copy(out=qp[:, c - 1, ts[0] : ts[-1] + 1, a : a + n], in_=b[:].rearrange("p (t r) -> p t r", r=n))

        def interleave_q(c, a, n):
            nc.vector.tensor_copy(
                out=qg[:, c, 4 * a : 4 * (a + n)].rearrange("p (r i t) -> p r t i", i=4, t=4),
                in_=qp[:, c - 1, :, a : a + n].rearrange("p t (r i) -> p r t i", i=4),
            )

        def quant_q(c, a, n):
            o = TOK * c + a
            nc.vector.quantize_mx(out=qc[:, o : o + n].bitcast(FP8X4), scales=qs[:, o : o + n], in_=qg[:, c, 4 * a : 4 * (a + n)])

        def transpose_q(pr):
            t = bank()
            for jj in range(2):
                words = ql[:, 2 * pr + jj, :].bitcast(F32)
                for u in range(2):
                    o = 256 * jj + 128 * u
                    nc.tensor.transpose(t[:, o : o + 128], words[:, 128 * u : 128 * (u + 1)], ident[:])
            return t

        def copy_q(pr, t):
            nc.vector.tensor_copy(
                out=qg[:, 0, 1024 * pr : 1024 * (pr + 1)].bitcast(F32).rearrange("p (j r u) -> p j r u", j=2, u=2),
                in_=t[:].rearrange("p (j u r) -> p j r u", j=2, u=2),
            )

        def qb_pass(t, j, w, sc, c):
            mm(t[:], qc, qs, TOK * c + 128 * j, w[:, c], sc[4 * c : P, :], c, c == 0, c == 2)

        def rope_mm(j, cs_, t=None):
            t = t or bank()
            for c in cs_:
                qb_pass(t, j, qbr, qbrs[:], c)
            return t

        def nope_mm(j, h, cs_, t=None):
            t = t or bank()
            for c in cs_:
                qb_pass(t, j, qbn[:, :, h, :], qbs[:, 640 * h + 128 : 640 * (h + 1)], c)
            return t

        def rope_q(j, t):
            r3 = t[:].rearrange("p (h d) -> p h d", h=HEADS)
            ta = tmp.tile([P, HEADS, 128], F32, name="ta", tag="ta")
            tb = tmp.tile([P, HEADS, 128], F32, name="tb", tag="tb")
            nc.vector.tensor_tensor(out=ta[:], in0=r3, in1=cs[:, j : j + 1, :].to_broadcast([P, HEADS, 128]), op=MULT)
            nc.vector.tensor_tensor(out=tb[:, :, 0:64], in0=r3[:, :, 64:128], in1=sn[:, j : j + 1, 0:64].to_broadcast([P, HEADS, 64]), op=MULT)
            nc.vector.tensor_tensor(out=tb[:, :, 64:128], in0=r3[:, :, 0:64], in1=sn[:, j : j + 1, 64:128].to_broadcast([P, HEADS, 64]), op=MULT)
            nc.vector.tensor_tensor(out=qr_o[:, j // 2, :, j % 2, :], in0=ta[:], in1=tb[:], op=ADD)

        def store_rope(q):
            nc.sync.dma_start(out=q_rope[0, :, 256 * q : 256 * (q + 1), :].rearrange("h (p e) d -> p h (e d)", e=2), in_=qr_o[:, q, :, :, :].rearrange("p h e d -> p h (e d)"))

        nope_rows = q_nope[0].rearrange("h (q p e) d -> q e p h d", q=2, e=2)

        def copy_nope(eng, j, h, t):
            if eng == "v":
                nc.vector.tensor_copy(out=qn_o[:, j, h, :], in_=t[:])
            else:
                nc.scalar.copy(out=qn_o[:, j, h, :], in_=t[:])

        def store_nope(j, h, n):
            nc.sync.dma_start(out=nope_rows[j // 2, j % 2, :, h : h + n, :], in_=qn_o[:, j, h : h + n, :])

        def rope_k():
            ra = tmp.tile([P, 4, 128], F32, name="ra", tag="ta")
            rb = tmp.tile([P, 4, 128], F32, name="rb", tag="tb")
            nc.vector.tensor_tensor(out=ra[:], in0=kvr_o[:, :, 0:128], in1=cs[:], op=MULT)
            nc.vector.tensor_tensor(out=rb[:, :, 0:64], in0=kvr_o[:, :, 64:128], in1=sn[:, :, 0:64], op=MULT)
            nc.vector.tensor_tensor(out=rb[:, :, 64:128], in0=kvr_o[:, :, 0:64], in1=sn[:, :, 64:128], op=MULT)
            nc.vector.tensor_tensor(out=kr_o[:], in0=ra[:], in1=rb[:], op=ADD)
            nc.sync.dma_start(out=k_rope[0].rearrange("(q p e) d -> p q (e d)", q=2, e=2), in_=kr_o[:].rearrange("p (q e) d -> p q (e d)", q=2))

        warm_up(7)
        for g in range(4):
            cast_x("v" if g % 2 == 0 else "s", 0, 512 * g, 512 * (g + 1))
        transpose_x(0, (0,))
        warm_up(1)
        transpose_x(0, (1,))
        warm_up(1)
        scale_x(0, 0)
        for g in range(4):
            cast_x("s", 1, 512 * g, 512 * (g + 1))
        transpose_x(1, (0,))
        scale_x(0, 1)
        quant_x(0, 0)
        scale_x(0, 2)
        quant_x(0, 1)
        scale_x(0, 3)
        quant_x(0, 2)
        scale_x(1, 0)
        quant_x(0, 3)
        kv_pass(0, (0, 1), True)
        transpose_x(1, (1,))
        cast_x("s", 2, 0, 1024)
        cast_x("s", 2, 1024, 2048)
        kv_pass(0, (2, 3), True)
        transpose_x(2)
        for g in range(1, 4):
            scale_x(1, g)
            quant_x(1, g - 1)
        scale_x(2, 0)
        quant_x(1, 3)
        cast_x("s", 3, 0, 1024)
        cast_x("s", 3, 1024, 2048)
        kv_pass(1, (0, 1, 2, 3), True)
        transpose_x(3)
        qa_tokens(0)
        for g in range(1, 4):
            scale_x(2, g)
            quant_x(2, g - 1)
        scale_x(3, 0)
        quant_x(2, 3)
        qa_tokens(1)
        kv_pass(2, (0, 1, 2, 3), False)
        qa_tokens(2)
        for g in range(1, 4):
            scale_x(3, g)
            quant_x(3, g - 1)
        permute_qa(1, (0,))
        quant_x(3, 3)
        permute_qa(1, (1, 2, 3))
        permute_qa(2, (0, 1, 2, 3))
        kv_pass(3, (0, 1, 2, 3), False)
        qa_tokens(3)
        nc.vector.tensor_copy(out=qbrs[:].rearrange("p (h n) -> p h n", h=HEADS).bitcast(I32), in_=qbs[:].rearrange("p (h n) -> p h n", h=HEADS)[:, :, 0:128].bitcast(I32))
        nc.sync.dma_start(out=kvn_rows[:, 0, :, :], in_=kvn_o[:, 0:2, :])
        for q in range(2):
            nc.sync.dma_start(out=v_rope[0, 256 * q : 256 * (q + 1), :].rearrange("(p e) d -> p e d", e=2), in_=kvr_o[:, 2 * q : 2 * q + 2, 128:256])
        rope_k()
        for t in (0, 2):
            qa_channels(1, (t, t + 1), 0, 256)
        ta0 = transpose_q(0)
        ta1 = transpose_q(1)
        for t in (0, 2):
            qa_channels(2, (t, t + 1), 0, 256)
        for t in (0, 2):
            qa_channels(1, (t, t + 1), 256, 256)
        copy_q(0, ta0)
        interleave_q(1, 0, 256)
        quant_q(0, 0, 256)
        copy_q(1, ta1)
        quant_q(1, 0, 256)
        quant_q(0, 256, 256)
        interleave_q(2, 0, 128)
        interleave_q(2, 128, 128)
        quant_q(2, 0, 128)
        quant_q(2, 128, 128)
        rope_q(0, rope_mm(0, (0, 1, 2)))
        interleave_q(1, 256, 256)
        rope_q(1, rope_mm(1, (0, 1, 2)))
        quant_q(1, 256, 256)

        def nope(j, h):
            copy_nope("v" if h == 2 else "s", j, h, nope_mm(j, h, (0, 1, 2)))
            if h % 2:
                store_nope(j, h - 1, 2)

        for h in range(HEADS):
            nope(0, h)
        store_rope(0)
        for t in (0, 2):
            qa_channels(2, (t, t + 1), 256, 256)
        nope(1, 0)
        nope(1, 1)
        interleave_q(2, 256, 128)
        interleave_q(2, 384, 128)
        quant_q(2, 256, 128)
        quant_q(2, 384, 128)
        nope(1, 2)
        rope_q(2, rope_mm(2, (0, 1, 2)))
        nope(1, 3)
        rope_q(3, rope_mm(3, (0, 1, 2)))
        nope(2, 0)
        nope(2, 1)
        store_rope(1)
        nope(2, 2)
        nope(2, 3)
        for h in range(HEADS):
            nope(3, h)
        kv_nope_late(2)
        kv_nope_late(3)
